import numpy as np
import ml_dtypes


def mxq(x, axis, fmt="e4m3"):
    dtype, down = {"e4m3": (ml_dtypes.float8_e4m3fn, 7), "e5m2": (ml_dtypes.float8_e5m2, 14)}[fmt]
    v = np.moveaxis(np.asarray(x, np.float32).astype(ml_dtypes.bfloat16).astype(np.float64), axis, -1)
    blocks = v.reshape(v.shape[:-1] + (-1, 32))
    amax = np.abs(blocks).max(-1, keepdims=True)
    byte = np.maximum(np.where(amax > 0, np.frexp(amax)[1] - 1 + 127, 0) - down, 1)
    scale = np.exp2(byte - 127.0)
    codes = (blocks / scale).astype(np.float32).astype(dtype).astype(np.float64)
    return np.moveaxis((codes * scale).reshape(v.shape), -1, axis)


WIDE = False


def mx_kscale(k):
    if not WIDE:
        return np.ones(k)
    levels = np.array([10, -10, 5, -5, 0])
    a = np.random.permutation(np.resize(levels, k // 512 * 4)).reshape(k // 512, 4)
    idx = np.arange(k)
    return np.exp2(a[idx // 512, idx % 128 // 32])


BF16 = ml_dtypes.bfloat16


def bf(x):
    return np.asarray(x, np.float32).astype(BF16)


def f64(x):
    return np.asarray(x).astype(np.float64)


B, S, H, HD = 8, 512, 512, 128
NH = H // HD
HALF = HD // 2
WS = 1.5 * (HD / H) ** 0.25 / np.sqrt(H)


def rotate_half(u):
    return np.concatenate((-u[..., HALF:], u[..., :HALF]), axis=-1)


def rope(u, c, s):
    u4 = u.reshape(B, S, NH, HD)
    return (u4 * c[None, :, None, :] + rotate_half(u4) * s[None, :, None, :]).reshape(B, S, H)


def setup_inputs():
    s = mx_kscale(H)
    t = np.tile(mx_kscale(H).reshape(NH, 2, HALF)[:, :1, :], (1, 2, 1)).reshape(H)
    return {"hidden_states": bf(np.random.standard_normal((B, S, H)) * s),
            "wq_deq": bf(np.random.standard_normal((H, H)) * WS * t[:, None] / s[None, :]),
            "wk_deq": bf(np.random.standard_normal((H, H)) * WS / t[:, None] / s[None, :]),
            "cos": bf(np.random.random((S, HD))),
            "sin": bf(np.random.random((S, HD))),
            "attention_mask": bf(np.random.standard_normal((1, S, S)) * 0.5)}


def reference(hidden_states, wq_deq, wk_deq, cos, sin, attention_mask):
    xq = mxq(f64(hidden_states), 2, "e4m3")
    q = xq @ mxq(f64(wq_deq), 1, "e4m3").T
    k = xq @ mxq(f64(wk_deq), 1, "e4m3").T
    q_rot = rope(q, f64(cos), f64(sin))
    k_rot = rope(k, f64(cos), f64(sin))
    scores = (mxq(q_rot, 2, "e4m3") @ mxq(k_rot, 2, "e4m3").transpose(0, 2, 1)) / np.sqrt(HD)
    return scores + f64(attention_mask)

@@ -1,0 +1,210 @@
+from contextlib import ExitStack
+import math
+
+import concourse.mybir as mybir
+from concourse.masks import make_identity
+
+F32 = mybir.dt.float32
+BF16 = mybir.dt.bfloat16
+U32 = mybir.dt.uint32
+U8 = mybir.dt.uint8
+FP8X4 = mybir.dt.float8_e4m3fn_x4
+MULT = mybir.AluOpType.mult
+ADD = mybir.AluOpType.add
+
+P = 128
+B, S, H, HD = 8, 512, 512, 128
+HALF = HD // 2
+CHUNKS = H // HD
+TILES = S // P
+UNITS = B * TILES
+PACK = 4
+SCORE_LAG = TILES + 1
+INV_SQRT_HD = 1.0 / math.sqrt(HD)
+
+FLOPS = 2 * (2 * B * S * H * H) + 2 * B * S * S * H
+
+
+def tile_llamaattention_pa_t_kernel(
+    tc, hidden_states, wq_deq, wk_deq, cos, sin, attention_mask, out
+):
+    nc = tc.nc
+    with ExitStack() as ctx:
+        keep = ctx.enter_context(tc.tile_pool(name="keep", bufs=1))
+        stage = ctx.enter_context(tc.tile_pool(name="stage", bufs=2))
+        products = ctx.enter_context(tc.tile_pool(name="products", bufs=3))
+        results = ctx.enter_context(tc.tile_pool(name="results", bufs=4))
+        psum = ctx.enter_context(tc.psum_pool(name="psum", bufs=1))
+        ctx.enter_context(tc.manual_schedule())
+
+        wq_rows = keep.tile([P, TILES, H], BF16)
+        wk_rows = keep.tile([P, TILES, H], BF16)
+        x_rows = [keep.tile([P, TILES, H], BF16, name="x_rows%d" % b) for b in range(B)]
+        cos_rows = keep.tile([P, TILES, HD], BF16)
+        sin_signed = keep.tile([P, TILES, HD], BF16)
+        mask_rows = keep.tile([P, TILES, S], BF16)
+
+        def load_x(b):
+            nc.sync.dma_start(
+                out=x_rows[b][:],
+                in_=hidden_states[b].rearrange("(t p) k -> p t k", p=P),
+            )
+
+        nc.sync.dma_start(out=wq_rows[:], in_=wq_deq.rearrange("(t p) k -> p t k", p=P))
+        nc.sync.dma_start(out=wk_rows[:], in_=wk_deq.rearrange("(t p) k -> p t k", p=P))
+        load_x(0)
+        nc.sync.dma_start(out=cos_rows[:], in_=cos.rearrange("(t p) f -> p t f", p=P))
+        nc.sync.dma_start(out=sin_signed[:], in_=sin.rearrange("(t p) f -> p t f", p=P))
+        load_x(1)
+        nc.sync.dma_start(out=mask_rows[:], in_=attention_mask[0].rearrange("(t p) k -> p t k", p=P))
+        for b in range(2, B):
+            load_x(b)
+
+        identity = keep.tile([P, P], F32)
+        make_identity(nc, identity[:])
+
+        def turn_two_tiles(words, grouped_words, copy_out):
+            bank = psum.tile([P, 2, 2, P], F32, tag="turn_or_scores", bufs=2)
+            for r in range(2):
+                for u in range(2):
+                    nc.tensor.transpose(bank[:, r, u, :], words[:, r, u * P : (u + 1) * P], identity[:])
+            copy_out(
+                out=grouped_words.rearrange("p (r n) u -> p r n u", r=2),
+                in_=bank[:].rearrange("p r u n -> p r n u"),
+            )
+
+        def quantise(pool, grouped, tag):
+            codes = pool.tile([P, 512], U32, tag=tag + "_codes", align_bytes=64)
+            scales = pool.tile([P, 512], U8, tag=tag + "_scales", align_bytes=64)
+            nc.vector.quantize_mx(
+                out=codes[:].bitcast(FP8X4),
+                scales=scales[:],
+                in_=grouped[:].rearrange("p n t -> p (n t)"),
+            )
+            return codes, scales
+
+        def mx_pass(acc, stationary, t, moving):
+            cols = slice(t * P, (t + 1) * P)
+            nc.tensor.matmul_mx(
+                out=acc,
+                lhsT=stationary[0][:, cols].bitcast(FP8X4),
+                lhsT_scale=stationary[1][:, cols],
+                rhs=moving[0][:].bitcast(FP8X4),
+                rhs_scale=moving[1][:],
+                start=True,
+                stop=True,
+            )
+
+        w_mx = {}
+        x_grouped = {}
+        x_mx = {}
+        raw = {}
+        rot_grouped = {}
+        rot_mx = {}
+
+        def turn_x(b, half):
+            if half == 0:
+                x_grouped[b] = stage.tile([P, S, PACK], BF16, name="x_grouped", tag="x_grouped", align_bytes=64)
+            first = 2 * half
+            turn_two_tiles(
+                x_rows[b][:].bitcast(F32)[:, first : first + 2, :],
+                x_grouped[b][:].bitcast(F32)[:, first * P : (first + 2) * P, :],
+                nc.scalar.copy,
+            )
+
+        def project(i):
+            b, t = divmod(i, TILES)
+            for name in ("q", "k"):
+                raw[name, i] = psum.tile([P, H], F32, name=name + "_raw", tag=name + "_raw", bufs=2)
+                mx_pass(raw[name, i][:], x_mx[b], t, w_mx[name])
+
+        def rope(name, i):
+            b, t = divmod(i, TILES)
+            low, high = slice(0, HALF), slice(HALF, HD)
+            u = raw[name, i][:].rearrange("p (c f) -> p c f", c=CHUNKS)
+            straight = products.tile([P, CHUNKS, HD], F32)
+            crossed = products.tile([P, CHUNKS, HD], F32)
+            nc.vector.tensor_tensor(
+                out=straight[:], in0=u, in1=cos_rows[:, t : t + 1, :].to_broadcast([P, CHUNKS, HD]), op=MULT
+            )
+            nc.vector.tensor_tensor(
+                out=crossed[:, :, low],
+                in0=u[:, :, high],
+                in1=sin_signed[:, t : t + 1, low].to_broadcast([P, CHUNKS, HALF]),
+                op=MULT,
+            )
+            nc.vector.tensor_tensor(
+                out=crossed[:, :, high],
+                in0=u[:, :, low],
+                in1=sin_signed[:, t : t + 1, high].to_broadcast([P, CHUNKS, HALF]),
+                op=MULT,
+            )
+            turned = psum.tile([P, CHUNKS, P], F32, tag=name + "_turned")
+            for c in range(CHUNKS):
+                nc.tensor.matmul(
+                    out=turned[:, c, :], lhsT=straight[:, c, :], rhs=identity[:],
+                    is_transpose=True, start=True, stop=False,
+                )
+                nc.tensor.matmul(
+                    out=turned[:, c, :], lhsT=crossed[:, c, :], rhs=identity[:],
+                    is_transpose=True, start=False, stop=True,
+                )
+            if t == 0:
+                rot_grouped[name, b] = stage.tile(
+                    [P, S, PACK], BF16, name=name + "_rot", tag=name + "_rot", align_bytes=64
+                )
+            nc.scalar.copy(
+                out=rot_grouped[name, b][:, t * P : (t + 1) * P, :],
+                in_=turned[:].rearrange("p c n -> p n c"),
+            )
+
+        def score_pass(j):
+            b, t = divmod(j, TILES)
+            scores = psum.tile([P, S], F32, tag="turn_or_scores", bufs=2)
+            mx_pass(scores[:], rot_mx["q", b], t, rot_mx["k", b])
+            return scores
+
+        def finish(j, scores):
+            b, t = divmod(j, TILES)
+            result = results.tile([P, S], F32)
+            nc.vector.scalar_tensor_tensor(
+                out=result[:], in0=scores[:], scalar=INV_SQRT_HD, in1=mask_rows[:, t, :], op0=MULT, op1=ADD
+            )
+            nc.sync.dma_start(out=out[b, t * P : (t + 1) * P, :], in_=result[:])
+
+        for name, rows in (("q", wq_rows), ("k", wk_rows)):
+            w_grouped = keep.tile([P, H, PACK], BF16, tag=name + "_w_grouped", align_bytes=64)
+            for first in (0, 2):
+                turn_two_tiles(
+                    rows[:].bitcast(F32)[:, first : first + 2, :],
+                    w_grouped[:].bitcast(F32)[:, first * P : (first + 2) * P, :],
+                    nc.vector.tensor_copy,
+                )
+            w_mx[name] = quantise(keep, w_grouped, name + "_w")
+        turn_x(0, 0)
+        turn_x(0, 1)
+        x_mx[0] = quantise(stage, x_grouped[0], "x")
+        nc.vector.tensor_scalar_mul(
+            out=sin_signed[:, :, 0:HALF], in0=sin_signed[:, :, 0:HALF], scalar1=-1.0
+        )
+        project(0)
+
+        for i in range(UNITS + SCORE_LAG):
+            b, t = divmod(i, TILES)
+            j = i - SCORE_LAG
+            if i + 1 < UNITS:
+                project(i + 1)
+            if j >= 0:
+                scores = score_pass(j)
+            if t < 2 and b + 1 < B:
+                turn_x(b + 1, t)
+            if i < UNITS:
+                rope("q", i)
+                rope("k", i)
+            if t == 0 and 1 <= b <= B:
+                rot_mx["q", b - 1] = quantise(stage, rot_grouped["q", b - 1], "q_rot")
+                rot_mx["k", b - 1] = quantise(stage, rot_grouped["k", b - 1], "k_rot")
+            if t == 2 and b + 1 < B:
+                x_mx[b + 1] = quantise(stage, x_grouped[b + 1], "x")
+            if j >= 0:
+                finish(j, scores)

@@ -167,9 +167,8 @@ def tile_llamaattention_pa_t_kernel(
         def finish(j, scores):
             b, t = divmod(j, TILES)
             result = results.tile([P, S], F32)
-            nc.vector.scalar_tensor_tensor(
-                out=result[:], in0=scores[:], scalar=INV_SQRT_HD, in1=mask_rows[:, t, :], op0=MULT, op1=ADD
-            )
+            nc.scalar.mul(out=result[:], in_=scores[:], mul=INV_SQRT_HD)
+            nc.gpsimd.tensor_tensor(out=result[:], in0=result[:], in1=mask_rows[:, t, :], op=ADD)
             nc.sync.dma_start(out=out[b, t * P : (t + 1) * P, :], in_=result[:])
 
         for name, rows in (("q", wq_rows), ("k", wk_rows)):
@@ -195,7 +194,7 @@ def tile_llamaattention_pa_t_kernel(
             if i + 1 < UNITS:
                 project(i + 1)
             if j >= 0:
-                scores = score_pass(j)
+                finish(j, score_pass(j))
             if t < 2 and b + 1 < B:
                 turn_x(b + 1, t)
             if i < UNITS:
@@ -206,5 +205,3 @@ def tile_llamaattention_pa_t_kernel(
                 rot_mx["k", b - 1] = quantise(stage, rot_grouped["k", b - 1], "k_rot")
             if t == 2 and b + 1 < B:
                 x_mx[b + 1] = quantise(stage, x_grouped[b + 1], "x")
-            if j >= 0:
-                finish(j, scores)

@@ -17,9 +17,11 @@ B, S, H, HD = 8, 512, 512, 128
 HALF = HD // 2
 CHUNKS = H // HD
 TILES = S // P
-UNITS = B * TILES
+PAIR = 2
 PACK = 4
-SCORE_LAG = TILES + 1
+PHASES = 2 * TILES // PAIR
+STEPS = B * PHASES
+SCORE_LAG = 2
 INV_SQRT_HD = 1.0 / math.sqrt(HD)
 
 FLOPS = 2 * (2 * B * S * H * H) + 2 * B * S * S * H
@@ -32,56 +34,62 @@ def tile_llamaattention_pa_t_kernel(
     with ExitStack() as ctx:
         keep = ctx.enter_context(tc.tile_pool(name="keep", bufs=1))
         stage = ctx.enter_context(tc.tile_pool(name="stage", bufs=2))
-        products = ctx.enter_context(tc.tile_pool(name="products", bufs=3))
+        products = ctx.enter_context(tc.tile_pool(name="products", bufs=4))
         results = ctx.enter_context(tc.tile_pool(name="results", bufs=4))
-        psum = ctx.enter_context(tc.psum_pool(name="psum", bufs=1))
+        psum = ctx.enter_context(tc.psum_pool(name="psum", bufs=2))
         ctx.enter_context(tc.manual_schedule())
 
-        wq_rows = keep.tile([P, TILES, H], BF16)
-        wk_rows = keep.tile([P, TILES, H], BF16)
+        w_rows = {name: keep.tile([P, TILES, H], BF16, name=name + "_w_rows") for name in ("k", "q")}
         x_rows = [keep.tile([P, TILES, H], BF16, name="x_rows%d" % b) for b in range(B)]
         cos_rows = keep.tile([P, TILES, HD], BF16)
         sin_signed = keep.tile([P, TILES, HD], BF16)
         mask_rows = keep.tile([P, TILES, S], BF16)
 
-        def load_x(b):
-            nc.sync.dma_start(
-                out=x_rows[b][:],
-                in_=hidden_states[b].rearrange("(t p) k -> p t k", p=P),
-            )
+        def load_tiles(rows, dram):
+            nc.sync.dma_start(out=rows[:], in_=dram.rearrange("(t p) k -> p t k", p=P))
 
-        nc.sync.dma_start(out=wq_rows[:], in_=wq_deq.rearrange("(t p) k -> p t k", p=P))
-        nc.sync.dma_start(out=wk_rows[:], in_=wk_deq.rearrange("(t p) k -> p t k", p=P))
-        load_x(0)
-        nc.sync.dma_start(out=cos_rows[:], in_=cos.rearrange("(t p) f -> p t f", p=P))
-        nc.sync.dma_start(out=sin_signed[:], in_=sin.rearrange("(t p) f -> p t f", p=P))
-        load_x(1)
-        nc.sync.dma_start(out=mask_rows[:], in_=attention_mask[0].rearrange("(t p) k -> p t k", p=P))
+        load_tiles(w_rows["k"], wk_deq)
+        load_tiles(x_rows[0], hidden_states[0])
+        load_tiles(w_rows["q"], wq_deq)
+        load_tiles(cos_rows, cos)
+        load_tiles(sin_signed, sin)
+        load_tiles(x_rows[1], hidden_states[1])
+        load_tiles(mask_rows, attention_mask[0])
         for b in range(2, B):
-            load_x(b)
+            load_tiles(x_rows[b], hidden_states[b])
 
         identity = keep.tile([P, P], F32)
         make_identity(nc, identity[:])
 
-        def turn_two_tiles(words, grouped_words, copy_out):
-            bank = psum.tile([P, 2, 2, P], F32, tag="turn_or_scores", bufs=2)
-            for r in range(2):
+        def new_grouped(pool, tag):
+            return pool.tile([P, 512, PACK], BF16, name=tag, tag=tag, align_bytes=64)
+
+        def new_mx(pool, tag):
+            codes = pool.tile([P, 512], U32, tag=tag + "_codes", align_bytes=64)
+            scales = pool.tile([P, 512], U8, tag=tag + "_scales", align_bytes=64)
+            return codes, scales
+
+        def pair_columns(first):
+            return slice(first * P, (first + PAIR) * P)
+
+        def turn_pair(rows, grouped, first):
+            words = rows[:].bitcast(F32)
+            bank = psum.tile([P, PAIR, 2, P], F32, tag="turn_or_scores")
+            for r in range(PAIR):
                 for u in range(2):
-                    nc.tensor.transpose(bank[:, r, u, :], words[:, r, u * P : (u + 1) * P], identity[:])
-            copy_out(
-                out=grouped_words.rearrange("p (r n) u -> p r n u", r=2),
+                    nc.tensor.transpose(bank[:, r, u, :], words[:, first + r, u * P : (u + 1) * P], identity[:])
+            nc.scalar.copy(
+                out=grouped[:].bitcast(F32)[:, pair_columns(first), :].rearrange("p (r n) u -> p r n u", r=PAIR),
                 in_=bank[:].rearrange("p r u n -> p r n u"),
             )
 
-        def quantise(pool, grouped, tag):
-            codes = pool.tile([P, 512], U32, tag=tag + "_codes", align_bytes=64)
-            scales = pool.tile([P, 512], U8, tag=tag + "_scales", align_bytes=64)
+        def quantise_pair(grouped, mx, first):
+            cols = pair_columns(first)
             nc.vector.quantize_mx(
-                out=codes[:].bitcast(FP8X4),
-                scales=scales[:],
-                in_=grouped[:].rearrange("p n t -> p (n t)"),
+                out=mx[0][:, cols].bitcast(FP8X4),
+                scales=mx[1][:, cols],
+                in_=grouped[:, cols, :].rearrange("p n t -> p (n t)"),
             )
-            return codes, scales
 
         def mx_pass(acc, stationary, t, moving):
             cols = slice(t * P, (t + 1) * P)
@@ -102,26 +110,27 @@ def tile_llamaattention_pa_t_kernel(
         rot_grouped = {}
         rot_mx = {}
 
-        def turn_x(b, half):
-            if half == 0:
-                x_grouped[b] = stage.tile([P, S, PACK], BF16, name="x_grouped", tag="x_grouped", align_bytes=64)
-            first = 2 * half
-            turn_two_tiles(
-                x_rows[b][:].bitcast(F32)[:, first : first + 2, :],
-                x_grouped[b][:].bitcast(F32)[:, first * P : (first + 2) * P, :],
-                nc.scalar.copy,
-            )
+        def work_of(s):
+            b, phase = divmod(s, PHASES)
+            return b, ("k", "k", "q", "q")[phase], PAIR * (phase % 2)
 
-        def project(i):
-            b, t = divmod(i, TILES)
-            for name in ("q", "k"):
-                raw[name, i] = psum.tile([P, H], F32, name=name + "_raw", tag=name + "_raw", bufs=2)
-                mx_pass(raw[name, i][:], x_mx[b], t, w_mx[name])
+        def turn_x(b, first):
+            if first == 0:
+                x_grouped[b] = new_grouped(stage, "x_grouped")
+                x_mx[b] = new_mx(stage, "x")
+            turn_pair(x_rows[b], x_grouped[b], first)
 
-        def rope(name, i):
-            b, t = divmod(i, TILES)
+        def project(s):
+            b, name, first = work_of(s)
+            for r in range(PAIR):
+                raw[s, r] = psum.tile([P, H], F32, name="raw", tag="raw", bufs=2 * PAIR)
+                mx_pass(raw[s, r][:], x_mx[b], first + r, w_mx[name])
+
+        def rope(s, r):
+            b, name, first = work_of(s)
+            t = first + r
             low, high = slice(0, HALF), slice(HALF, HD)
-            u = raw[name, i][:].rearrange("p (c f) -> p c f", c=CHUNKS)
+            u = raw[s, r][:].rearrange("p (c f) -> p c f", c=CHUNKS)
             straight = products.tile([P, CHUNKS, HD], F32)
             crossed = products.tile([P, CHUNKS, HD], F32)
             nc.vector.tensor_tensor(
@@ -139,7 +148,7 @@ def tile_llamaattention_pa_t_kernel(
                 in1=sin_signed[:, t : t + 1, high].to_broadcast([P, CHUNKS, HALF]),
                 op=MULT,
             )
-            turned = psum.tile([P, CHUNKS, P], F32, tag=name + "_turned")
+            turned = psum.tile([P, CHUNKS, P], F32)
             for c in range(CHUNKS):
                 nc.tensor.matmul(
                     out=turned[:, c, :], lhsT=straight[:, c, :], rhs=identity[:],
@@ -150,58 +159,58 @@ def tile_llamaattention_pa_t_kernel(
                     is_transpose=True, start=False, stop=True,
                 )
             if t == 0:
-                rot_grouped[name, b] = stage.tile(
-                    [P, S, PACK], BF16, name=name + "_rot", tag=name + "_rot", align_bytes=64
-                )
+                rot_grouped[name, b] = new_grouped(stage, name + "_rot_grouped")
+                rot_mx[name, b] = new_mx(stage, name + "_rot")
             nc.scalar.copy(
                 out=rot_grouped[name, b][:, t * P : (t + 1) * P, :],
                 in_=turned[:].rearrange("p c n -> p n c"),
             )
 
-        def score_pass(j):
-            b, t = divmod(j, TILES)
-            scores = psum.tile([P, S], F32, tag="turn_or_scores", bufs=2)
-            mx_pass(scores[:], rot_mx["q", b], t, rot_mx["k", b])
-            return scores
+        def quantise_rope(s):
+            b, name, first = work_of(s)
+            quantise_pair(rot_grouped[name, b], rot_mx[name, b], first)
 
-        def finish(j, scores):
-            b, t = divmod(j, TILES)
+        def scores_of(s, r):
+            b, name, first = work_of(s)
+            t = first + r
+            scores = psum.tile([P, S], F32, tag="turn_or_scores")
+            mx_pass(scores[:], rot_mx["q", b], t, rot_mx["k", b])
             result = results.tile([P, S], F32)
             nc.scalar.mul(out=result[:], in_=scores[:], mul=INV_SQRT_HD)
             nc.gpsimd.tensor_tensor(out=result[:], in0=result[:], in1=mask_rows[:, t, :], op=ADD)
             nc.sync.dma_start(out=out[b, t * P : (t + 1) * P, :], in_=result[:])
 
-        for name, rows in (("q", wq_rows), ("k", wk_rows)):
-            w_grouped = keep.tile([P, H, PACK], BF16, tag=name + "_w_grouped", align_bytes=64)
-            for first in (0, 2):
-                turn_two_tiles(
-                    rows[:].bitcast(F32)[:, first : first + 2, :],
-                    w_grouped[:].bitcast(F32)[:, first * P : (first + 2) * P, :],
-                    nc.vector.tensor_copy,
-                )
-            w_mx[name] = quantise(keep, w_grouped, name + "_w")
-        turn_x(0, 0)
-        turn_x(0, 1)
-        x_mx[0] = quantise(stage, x_grouped[0], "x")
+        def prepare_weight(name):
+            w_grouped = new_grouped(keep, name + "_w_grouped")
+            w_mx[name] = new_mx(keep, name + "_w")
+            for first in range(0, TILES, PAIR):
+                turn_pair(w_rows[name], w_grouped, first)
+                quantise_pair(w_grouped, w_mx[name], first)
+
+        prepare_weight("k")
+        for first in range(0, TILES, PAIR):
+            turn_x(0, first)
+            quantise_pair(x_grouped[0], x_mx[0], first)
+        prepare_weight("q")
         nc.vector.tensor_scalar_mul(
             out=sin_signed[:, :, 0:HALF], in0=sin_signed[:, :, 0:HALF], scalar1=-1.0
         )
         project(0)
 
-        for i in range(UNITS + SCORE_LAG):
-            b, t = divmod(i, TILES)
-            j = i - SCORE_LAG
-            if i + 1 < UNITS:
-                project(i + 1)
-            if j >= 0:
-                finish(j, score_pass(j))
-            if t < 2 and b + 1 < B:
-                turn_x(b + 1, t)
-            if i < UNITS:
-                rope("q", i)
-                rope("k", i)
-            if t == 0 and 1 <= b <= B:
-                rot_mx["q", b - 1] = quantise(stage, rot_grouped["q", b - 1], "q_rot")
-                rot_mx["k", b - 1] = quantise(stage, rot_grouped["k", b - 1], "k_rot")
-            if t == 2 and b + 1 < B:
-                x_mx[b + 1] = quantise(stage, x_grouped[b + 1], "x")
+        for s in range(STEPS + SCORE_LAG):
+            b, phase = divmod(s, PHASES)
+            next_x = PAIR * (phase - 2)
+            if s + 1 < STEPS:
+                project(s + 1)
+            if s >= SCORE_LAG and work_of(s - SCORE_LAG)[1] == "q":
+                scores_of(s - SCORE_LAG, 0)
+                scores_of(s - SCORE_LAG, 1)
+            if next_x >= 0 and b + 1 < B:
+                turn_x(b + 1, next_x)
+            if s < STEPS:
+                rope(s, 0)
+                rope(s, 1)
+            if 1 <= s <= STEPS:
+                quantise_rope(s - 1)
+            if next_x >= 0 and b + 1 < B:
+                quantise_pair(x_grouped[b + 1], x_mx[b + 1], next_x)

@@ -17,11 +17,10 @@ B, S, H, HD = 8, 512, 512, 128
 HALF = HD // 2
 CHUNKS = H // HD
 TILES = S // P
+UNITS = B * TILES
 PAIR = 2
 PACK = 4
-PHASES = 2 * TILES // PAIR
-STEPS = B * PHASES
-SCORE_LAG = 2
+SCORE_TILES = ((), (0, 1), (2,), (3,))
 INV_SQRT_HD = 1.0 / math.sqrt(HD)
 
 FLOPS = 2 * (2 * B * S * H * H) + 2 * B * S * S * H
@@ -48,9 +47,9 @@ def tile_llamaattention_pa_t_kernel(
         def load_tiles(rows, dram):
             nc.sync.dma_start(out=rows[:], in_=dram.rearrange("(t p) k -> p t k", p=P))
 
+        load_tiles(w_rows["q"], wq_deq)
         load_tiles(w_rows["k"], wk_deq)
         load_tiles(x_rows[0], hidden_states[0])
-        load_tiles(w_rows["q"], wq_deq)
         load_tiles(cos_rows, cos)
         load_tiles(sin_signed, sin)
         load_tiles(x_rows[1], hidden_states[1])
@@ -83,13 +82,14 @@ def tile_llamaattention_pa_t_kernel(
                 in_=bank[:].rearrange("p r u n -> p r n u"),
             )
 
-        def quantise_pair(grouped, mx, first):
-            cols = pair_columns(first)
+        def quantise(pool, grouped, tag):
+            mx = new_mx(pool, tag)
             nc.vector.quantize_mx(
-                out=mx[0][:, cols].bitcast(FP8X4),
-                scales=mx[1][:, cols],
-                in_=grouped[:, cols, :].rearrange("p n t -> p (n t)"),
+                out=mx[0][:].bitcast(FP8X4),
+                scales=mx[1][:],
+                in_=grouped[:].rearrange("p n t -> p (n t)"),
             )
+            return mx
 
         def mx_pass(acc, stationary, t, moving):
             cols = slice(t * P, (t + 1) * P)
@@ -110,27 +110,21 @@ def tile_llamaattention_pa_t_kernel(
         rot_grouped = {}
         rot_mx = {}
 
-        def work_of(s):
-            b, phase = divmod(s, PHASES)
-            return b, ("k", "k", "q", "q")[phase], PAIR * (phase % 2)
-
         def turn_x(b, first):
             if first == 0:
                 x_grouped[b] = new_grouped(stage, "x_grouped")
-                x_mx[b] = new_mx(stage, "x")
             turn_pair(x_rows[b], x_grouped[b], first)
 
-        def project(s):
-            b, name, first = work_of(s)
-            for r in range(PAIR):
-                raw[s, r] = psum.tile([P, H], F32, name="raw", tag="raw", bufs=2 * PAIR)
-                mx_pass(raw[s, r][:], x_mx[b], first + r, w_mx[name])
+        def project(i):
+            b, t = divmod(i, TILES)
+            for name in ("q", "k"):
+                raw[name, i] = psum.tile([P, H], F32, name="raw", tag="raw", bufs=4)
+                mx_pass(raw[name, i][:], x_mx[b], t, w_mx[name])
 
-        def rope(s, r):
-            b, name, first = work_of(s)
-            t = first + r
+        def rope(name, i):
+            b, t = divmod(i, TILES)
             low, high = slice(0, HALF), slice(HALF, HD)
-            u = raw[s, r][:].rearrange("p (c f) -> p c f", c=CHUNKS)
+            u = raw[name, i][:].rearrange("p (c f) -> p c f", c=CHUNKS)
             straight = products.tile([P, CHUNKS, HD], F32)
             crossed = products.tile([P, CHUNKS, HD], F32)
             nc.vector.tensor_tensor(
@@ -160,57 +154,54 @@ def tile_llamaattention_pa_t_kernel(
                 )
             if t == 0:
                 rot_grouped[name, b] = new_grouped(stage, name + "_rot_grouped")
-                rot_mx[name, b] = new_mx(stage, name + "_rot")
             nc.scalar.copy(
                 out=rot_grouped[name, b][:, t * P : (t + 1) * P, :],
                 in_=turned[:].rearrange("p c n -> p n c"),
             )
 
-        def quantise_rope(s):
-            b, name, first = work_of(s)
-            quantise_pair(rot_grouped[name, b], rot_mx[name, b], first)
-
-        def scores_of(s, r):
-            b, name, first = work_of(s)
-            t = first + r
+        def scores_of(b, t):
             scores = psum.tile([P, S], F32, tag="turn_or_scores")
             mx_pass(scores[:], rot_mx["q", b], t, rot_mx["k", b])
             result = results.tile([P, S], F32)
-            nc.scalar.mul(out=result[:], in_=scores[:], mul=INV_SQRT_HD)
-            nc.gpsimd.tensor_tensor(out=result[:], in0=result[:], in1=mask_rows[:, t, :], op=ADD)
+            if b < B - 1:
+                nc.scalar.mul(out=result[:], in_=scores[:], mul=INV_SQRT_HD)
+                nc.gpsimd.tensor_tensor(out=result[:], in0=result[:], in1=mask_rows[:, t, :], op=ADD)
+            else:
+                nc.vector.scalar_tensor_tensor(
+                    out=result[:], in0=scores[:], scalar=INV_SQRT_HD, in1=mask_rows[:, t, :], op0=MULT, op1=ADD
+                )
             nc.sync.dma_start(out=out[b, t * P : (t + 1) * P, :], in_=result[:])
 
-        def prepare_weight(name):
+        for name in ("q", "k"):
             w_grouped = new_grouped(keep, name + "_w_grouped")
-            w_mx[name] = new_mx(keep, name + "_w")
             for first in range(0, TILES, PAIR):
                 turn_pair(w_rows[name], w_grouped, first)
-                quantise_pair(w_grouped, w_mx[name], first)
-
-        prepare_weight("k")
+            w_mx[name] = quantise(keep, w_grouped, name + "_w")
         for first in range(0, TILES, PAIR):
             turn_x(0, first)
-            quantise_pair(x_grouped[0], x_mx[0], first)
-        prepare_weight("q")
+        x_mx[0] = quantise(stage, x_grouped[0], "x")
         nc.vector.tensor_scalar_mul(
             out=sin_signed[:, :, 0:HALF], in0=sin_signed[:, :, 0:HALF], scalar1=-1.0
         )
         project(0)
+        turn_x(1, 0)
 
-        for s in range(STEPS + SCORE_LAG):
-            b, phase = divmod(s, PHASES)
-            next_x = PAIR * (phase - 2)
-            if s + 1 < STEPS:
-                project(s + 1)
-            if s >= SCORE_LAG and work_of(s - SCORE_LAG)[1] == "q":
-                scores_of(s - SCORE_LAG, 0)
-                scores_of(s - SCORE_LAG, 1)
-            if next_x >= 0 and b + 1 < B:
-                turn_x(b + 1, next_x)
-            if s < STEPS:
-                rope(s, 0)
-                rope(s, 1)
-            if 1 <= s <= STEPS:
-                quantise_rope(s - 1)
-            if next_x >= 0 and b + 1 < B:
-                quantise_pair(x_grouped[b + 1], x_mx[b + 1], next_x)
+        for i in range(UNITS + TILES):
+            b, t = divmod(i, TILES)
+            if i + 1 < UNITS:
+                project(i + 1)
+            if b >= 1:
+                for score_tile in SCORE_TILES[t]:
+                    scores_of(b - 1, score_tile)
+            if t == TILES - 1 and b + 2 < B:
+                turn_x(b + 2, 0)
+            if t == 0 and b + 1 < B:
+                turn_x(b + 1, PAIR)
+            if i < UNITS:
+                rope("q", i)
+                rope("k", i)
+            if t == 0 and b >= 1:
+                rot_mx["q", b - 1] = quantise(stage, rot_grouped["q", b - 1], "q_rot")
+                rot_mx["k", b - 1] = quantise(stage, rot_grouped["k", b - 1], "k_rot")
+            if t == 0 and b + 1 < B:
+                x_mx[b + 1] = quantise(stage, x_grouped[b + 1], "x")

from contextlib import ExitStack
import math

import concourse.mybir as mybir
from concourse.masks import make_identity

F32 = mybir.dt.float32
BF16 = mybir.dt.bfloat16
U32 = mybir.dt.uint32
U8 = mybir.dt.uint8
FP8X4 = mybir.dt.float8_e4m3fn_x4
MULT = mybir.AluOpType.mult
ADD = mybir.AluOpType.add

P = 128
B, S, H, HD = 8, 512, 512, 128
HALF = HD // 2
CHUNKS = H // HD
TILES = S // P
UNITS = B * TILES
PAIR = 2
PACK = 4
SCORE_TILES = ((), (0, 1), (2,), (3,))
INV_SQRT_HD = 1.0 / math.sqrt(HD)

FLOPS = 2 * (2 * B * S * H * H) + 2 * B * S * S * H


def tile_llamaattention_pa_t_kernel(
    tc, hidden_states, wq_deq, wk_deq, cos, sin, attention_mask, out
):
    nc = tc.nc
    with ExitStack() as ctx:
        keep = ctx.enter_context(tc.tile_pool(name="keep", bufs=1))
        stage = ctx.enter_context(tc.tile_pool(name="stage", bufs=2))
        products = ctx.enter_context(tc.tile_pool(name="products", bufs=4))
        results = ctx.enter_context(tc.tile_pool(name="results", bufs=4))
        psum = ctx.enter_context(tc.psum_pool(name="psum", bufs=2))
        ctx.enter_context(tc.manual_schedule())

        w_rows = {name: keep.tile([P, TILES, H], BF16, name=name + "_w_rows") for name in ("k", "q")}
        x_rows = [keep.tile([P, TILES, H], BF16, name="x_rows%d" % b) for b in range(B)]
        cos_rows = keep.tile([P, TILES, HD], BF16)
        sin_signed = keep.tile([P, TILES, HD], BF16)
        mask_rows = keep.tile([P, TILES, S], BF16)

        def load_tiles(rows, dram):
            nc.sync.dma_start(out=rows[:], in_=dram.rearrange("(t p) k -> p t k", p=P))

        load_tiles(w_rows["q"], wq_deq)
        load_tiles(w_rows["k"], wk_deq)
        load_tiles(x_rows[0], hidden_states[0])
        load_tiles(cos_rows, cos)
        load_tiles(sin_signed, sin)
        load_tiles(x_rows[1], hidden_states[1])
        load_tiles(mask_rows, attention_mask[0])
        for b in range(2, B):
            load_tiles(x_rows[b], hidden_states[b])

        identity = keep.tile([P, P], F32)
        make_identity(nc, identity[:])

        def new_grouped(pool, tag):
            return pool.tile([P, 512, PACK], BF16, name=tag, tag=tag, align_bytes=64)

        def new_mx(pool, tag):
            codes = pool.tile([P, 512], U32, tag=tag + "_codes", align_bytes=64)
            scales = pool.tile([P, 512], U8, tag=tag + "_scales", align_bytes=64)
            return codes, scales

        def pair_columns(first):
            return slice(first * P, (first + PAIR) * P)

        def turn_pair(rows, grouped, first):
            words = rows[:].bitcast(F32)
            bank = psum.tile([P, PAIR, 2, P], F32, tag="turn_or_scores")
            for r in range(PAIR):
                for u in range(2):
                    nc.tensor.transpose(bank[:, r, u, :], words[:, first + r, u * P : (u + 1) * P], identity[:])
            nc.scalar.copy(
                out=grouped[:].bitcast(F32)[:, pair_columns(first), :].rearrange("p (r n) u -> p r n u", r=PAIR),
                in_=bank[:].rearrange("p r u n -> p r n u"),
            )

        def quantise(pool, grouped, tag):
            mx = new_mx(pool, tag)
            nc.vector.quantize_mx(
                out=mx[0][:].bitcast(FP8X4),
                scales=mx[1][:],
                in_=grouped[:].rearrange("p n t -> p (n t)"),
            )
            return mx

        def mx_pass(acc, stationary, t, moving):
            cols = slice(t * P, (t + 1) * P)
            nc.tensor.matmul_mx(
                out=acc,
                lhsT=stationary[0][:, cols].bitcast(FP8X4),
                lhsT_scale=stationary[1][:, cols],
                rhs=moving[0][:].bitcast(FP8X4),
                rhs_scale=moving[1][:],
                start=True,
                stop=True,
            )

        w_mx = {}
        x_grouped = {}
        x_mx = {}
        raw = {}
        rot_grouped = {}
        rot_mx = {}

        def turn_x(b, first):
            if first == 0:
                x_grouped[b] = new_grouped(stage, "x_grouped")
            turn_pair(x_rows[b], x_grouped[b], first)

        def project(i):
            b, t = divmod(i, TILES)
            for name in ("q", "k"):
                raw[name, i] = psum.tile([P, H], F32, name="raw", tag="raw", bufs=4)
                mx_pass(raw[name, i][:], x_mx[b], t, w_mx[name])

        def rope(name, i):
            b, t = divmod(i, TILES)
            low, high = slice(0, HALF), slice(HALF, HD)
            u = raw[name, i][:].rearrange("p (c f) -> p c f", c=CHUNKS)
            straight = products.tile([P, CHUNKS, HD], F32)
            crossed = products.tile([P, CHUNKS, HD], F32)
            nc.vector.tensor_tensor(
                out=straight[:], in0=u, in1=cos_rows[:, t : t + 1, :].to_broadcast([P, CHUNKS, HD]), op=MULT
            )
            nc.vector.tensor_tensor(
                out=crossed[:, :, low],
                in0=u[:, :, high],
                in1=sin_signed[:, t : t + 1, low].to_broadcast([P, CHUNKS, HALF]),
                op=MULT,
            )
            nc.vector.tensor_tensor(
                out=crossed[:, :, high],
                in0=u[:, :, low],
                in1=sin_signed[:, t : t + 1, high].to_broadcast([P, CHUNKS, HALF]),
                op=MULT,
            )
            turned = psum.tile([P, CHUNKS, P], F32)
            for c in range(CHUNKS):
                nc.tensor.matmul(
                    out=turned[:, c, :], lhsT=straight[:, c, :], rhs=identity[:],
                    is_transpose=True, start=True, stop=False,
                )
                nc.tensor.matmul(
                    out=turned[:, c, :], lhsT=crossed[:, c, :], rhs=identity[:],
                    is_transpose=True, start=False, stop=True,
                )
            if t == 0:
                rot_grouped[name, b] = new_grouped(stage, name + "_rot_grouped")
            nc.scalar.copy(
                out=rot_grouped[name, b][:, t * P : (t + 1) * P, :],
                in_=turned[:].rearrange("p c n -> p n c"),
            )

        def scores_of(b, t):
            scores = psum.tile([P, S], F32, tag="turn_or_scores")
            mx_pass(scores[:], rot_mx["q", b], t, rot_mx["k", b])
            result = results.tile([P, S], F32)
            if b < B - 1:
                nc.scalar.mul(out=result[:], in_=scores[:], mul=INV_SQRT_HD)
                nc.gpsimd.tensor_tensor(out=result[:], in0=result[:], in1=mask_rows[:, t, :], op=ADD)
            else:
                nc.vector.scalar_tensor_tensor(
                    out=result[:], in0=scores[:], scalar=INV_SQRT_HD, in1=mask_rows[:, t, :], op0=MULT, op1=ADD
                )
            nc.sync.dma_start(out=out[b, t * P : (t + 1) * P, :], in_=result[:])

        for name in ("q", "k"):
            w_grouped = new_grouped(keep, name + "_w_grouped")
            for first in range(0, TILES, PAIR):
                turn_pair(w_rows[name], w_grouped, first)
            w_mx[name] = quantise(keep, w_grouped, name + "_w")
        for first in range(0, TILES, PAIR):
            turn_x(0, first)
        x_mx[0] = quantise(stage, x_grouped[0], "x")
        nc.vector.tensor_scalar_mul(
            out=sin_signed[:, :, 0:HALF], in0=sin_signed[:, :, 0:HALF], scalar1=-1.0
        )
        project(0)
        turn_x(1, 0)

        for i in range(UNITS + TILES):
            b, t = divmod(i, TILES)
            if i + 1 < UNITS:
                project(i + 1)
            if b >= 1:
                for score_tile in SCORE_TILES[t]:
                    scores_of(b - 1, score_tile)
            if t == TILES - 1 and b + 2 < B:
                turn_x(b + 2, 0)
            if t == 0 and b + 1 < B:
                turn_x(b + 1, PAIR)
            if i < UNITS:
                rope("q", i)
                rope("k", i)
            if t == 0 and b >= 1:
                rot_mx["q", b - 1] = quantise(stage, rot_grouped["q", b - 1], "q_rot")
                rot_mx["k", b - 1] = quantise(stage, rot_grouped["k", b - 1], "k_rot")
            if t == 0 and b + 1 < B:
                x_mx[b + 1] = quantise(stage, x_grouped[b + 1], "x")
